import numpy as np
import ml_dtypes


def mxq(x, axis, fmt="e4m3"):
    dtype, down = {"e4m3": (ml_dtypes.float8_e4m3fn, 7), "e5m2": (ml_dtypes.float8_e5m2, 14)}[fmt]
    v = np.moveaxis(np.asarray(x, np.float32).astype(ml_dtypes.bfloat16).astype(np.float64), axis, -1)
    blocks = v.reshape(v.shape[:-1] + (-1, 32))
    amax = np.abs(blocks).max(-1, keepdims=True)
    byte = np.maximum(np.where(amax > 0, np.frexp(amax)[1] - 1 + 127, 0) - down, 1)
    scale = np.exp2(byte - 127.0)
    codes = (blocks / scale).astype(np.float32).astype(dtype).astype(np.float64)
    return np.moveaxis((codes * scale).reshape(v.shape), -1, axis)


WIDE = False


def mx_kscale(k):
    if not WIDE:
        return np.ones(k)
    levels = np.array([10, -10, 5, -5, 0])
    if k % 512:
        return np.exp2(np.random.permutation(np.resize(levels, k // 32))).repeat(32)
    a = np.empty((k // 512, 16))
    for p in range(k // 512):
        a[p, :8] = np.random.permutation(np.resize(levels, 8))
        for g in range(8):
            far = levels[np.abs(levels - a[p, g]) >= 10]
            a[p, g + 8] = far[np.random.randint(len(far))]
    return np.exp2(a.ravel()).repeat(32)


BF16 = ml_dtypes.bfloat16


def bf(x):
    return np.asarray(x, np.float32).astype(BF16)


def f64(x):
    return np.asarray(x).astype(np.float64)


B, N, D, H, DK, P = 4, 2048, 512, 2, 128, 512
E = H * DK


def setup_inputs():
    s = mx_kscale(D)
    return {"Q": bf(np.random.standard_normal((B, N, D)) * s),
            "WQ": bf(np.random.standard_normal((E, D)) * 1.5 / np.sqrt(D) / s)}


def reference(Q, WQ):
    q = mxq(f64(Q), 2, "e4m3") @ mxq(f64(WQ), 1, "e4m3").T
    q = q.reshape(B, N, H, DK).transpose(0, 2, 1, 3)
    g = np.exp(q - q.max(-1, keepdims=True))
    return g / g.sum(-1, keepdims=True)

@@ -1,0 +1,204 @@
+from contextlib import ExitStack
+
+import concourse.mybir as mybir
+from concourse.masks import make_identity
+
+F32 = mybir.dt.float32
+BF16 = mybir.dt.bfloat16
+U32 = mybir.dt.uint32
+U8 = mybir.dt.uint8
+FP8X4 = mybir.dt.float8_e4m3fn_x4
+
+P = 128
+PACK = 4
+HALVES = 2
+TOKENS = 4 * 2048
+BATCH_TOKENS = 2048
+K = 512
+HEADS = 2
+HEAD_DIM = 128
+FEATURES = HEADS * HEAD_DIM
+TILES = 4
+TILES_PER_BANK = 2
+BANKS = TILES // TILES_PER_BANK
+GROUP_TOKENS = TILES * P
+GROUPS = TOKENS // GROUP_TOKENS
+COPY_CYCLE = 4
+
+FLOPS = 2 * TOKENS * FEATURES * K
+
+
+def tile_multiheadattention_pb_t_kernel(tc, Q, WQ, out):
+    nc = tc.nc
+    with ExitStack() as ctx:
+        const = ctx.enter_context(tc.tile_pool(name="const", bufs=1))
+        rows_pool = ctx.enter_context(tc.tile_pool(name="rows", bufs=GROUPS))
+        operand_pool = ctx.enter_context(tc.tile_pool(name="operand", bufs=3))
+        stats_pool = ctx.enter_context(tc.tile_pool(name="stats", bufs=4))
+        probs_pool = ctx.enter_context(tc.tile_pool(name="probs", bufs=4))
+        flipped_pool = ctx.enter_context(tc.psum_pool(name="flipped", bufs=BANKS))
+        logits_pool = ctx.enter_context(tc.psum_pool(name="logits", bufs=3 * BANKS))
+        ctx.enter_context(tc.manual_schedule())
+
+        w_rows = const.tile([P, HEADS * K], BF16)
+        nc.sync.dma_start(
+            out=w_rows[:].rearrange("p (h k) -> p h k", h=HEADS),
+            in_=WQ.rearrange("(h p) k -> p h k", p=P),
+        )
+        q_groups = Q.flatten_outer_dims().rearrange("(g p t) k -> g p (t k)", p=P, t=TILES)
+        q_rows = []
+        for g in range(GROUPS):
+            rows = rows_pool.tile([P, TILES * K], BF16)
+            nc.sync.dma_start(out=rows[:], in_=q_groups[g])
+            q_rows.append(rows)
+
+        ident = const.tile([P, P], F32)
+        make_identity(nc, ident[:])
+
+        warm = const.tile([P, 1], F32)
+        nc.vector.memset(warm[:], 0.0)
+        nc.scalar.activation(out=warm[:], in_=warm[:], func=mybir.ActivationFunctionType.Exp)
+
+        def flip(rows, n_tiles):
+            words = rows[:].bitcast(F32).rearrange("p (j w) -> p j w", j=n_tiles)
+            banks = []
+            for first in range(0, n_tiles, TILES_PER_BANK):
+                flipped = flipped_pool.tile([P, TILES_PER_BANK, HALVES, P], F32)
+                for j in range(TILES_PER_BANK):
+                    for u in range(HALVES):
+                        nc.tensor.transpose(
+                            flipped[:, j, u, :],
+                            words[:, first + j, u :: HALVES],
+                            ident[:],
+                        )
+                banks.append(flipped)
+            return banks
+
+        def lay_side_by_side(banks, grouped, first_bank):
+            grouped_words = grouped[:].bitcast(F32).rearrange(
+                "p (i j r u) -> p i j r u", i=len(banks), j=TILES_PER_BANK, u=HALVES
+            )
+            for i, flipped in enumerate(banks):
+                if (first_bank + i) % COPY_CYCLE == 1:
+                    copy_out = nc.vector.tensor_copy
+                else:
+                    copy_out = nc.scalar.copy
+                copy_out(out=grouped_words[:, i], in_=flipped[:].rearrange("p j u r -> p j r u"))
+
+        w_grouped = const.tile([P, FEATURES * PACK], BF16, align_bytes=64)
+        w_codes = const.tile([P, FEATURES], U32, align_bytes=64)
+        w_scales = const.tile([P, FEATURES], U8, align_bytes=64)
+        lay_side_by_side(flip(w_rows, HEADS), w_grouped, 0)
+        nc.vector.quantize_mx(out=w_codes[:].bitcast(FP8X4), scales=w_scales[:], in_=w_grouped[:])
+
+        flipped_of = {}
+        grouped_of = {}
+        codes_of = {}
+        logits_of = {}
+        neg_max_of = {}
+        sums_of = {}
+        probs_of = {}
+        inverse_of = {}
+
+        def stage_flip(g):
+            flipped_of[g] = flip(q_rows[g], TILES)
+
+        def stage_copy(g):
+            grouped = operand_pool.tile([P, GROUP_TOKENS * PACK], BF16, align_bytes=64)
+            lay_side_by_side(flipped_of[g], grouped, g * BANKS)
+            grouped_of[g] = grouped
+
+        def stage_project(g):
+            codes = operand_pool.tile([P, GROUP_TOKENS], U32, align_bytes=64)
+            scales = operand_pool.tile([P, GROUP_TOKENS], U8, align_bytes=64)
+            nc.vector.quantize_mx(
+                out=codes[:].bitcast(FP8X4), scales=scales[:], in_=grouped_of[g][:]
+            )
+            banks = []
+            for first in range(0, TILES, TILES_PER_BANK):
+                logits = logits_pool.tile([P, TILES_PER_BANK, FEATURES], F32)
+                for j in range(TILES_PER_BANK):
+                    tokens = slice((first + j) * P, (first + j + 1) * P)
+                    nc.tensor.matmul_mx(
+                        out=logits[:, j, :],
+                        lhsT=codes[:, tokens].bitcast(FP8X4),
+                        lhsT_scale=scales[:, tokens],
+                        rhs=w_codes[:].bitcast(FP8X4),
+                        rhs_scale=w_scales[:],
+                        start=True,
+                        stop=True,
+                    )
+                banks.append(logits)
+            logits_of[g] = banks
+
+        def stage_max(g):
+            neg_max = stats_pool.tile([P, TILES * HEADS], F32)
+            per_bank = TILES_PER_BANK * HEADS
+            for i, logits in enumerate(logits_of[g]):
+                nc.vector.tensor_reduce(
+                    out=neg_max[:, i * per_bank : (i + 1) * per_bank],
+                    in_=logits[:].rearrange("p j (h d) -> p (j h) d", h=HEADS),
+                    axis=mybir.AxisListType.X,
+                    op=mybir.AluOpType.max,
+                    negate=True,
+                )
+            neg_max_of[g] = neg_max
+
+        def stage_exp(g):
+            probs = probs_pool.tile([P, HEADS, TILES, HEAD_DIM], F32)
+            sums = stats_pool.tile([P, TILES * HEADS], F32)
+            for t in range(TILES):
+                logits = logits_of[g][t // TILES_PER_BANK]
+                for h in range(HEADS):
+                    col = t * HEADS + h
+                    nc.scalar.activation(
+                        out=probs[:, h, t, :],
+                        in_=logits[:, t % TILES_PER_BANK, h * HEAD_DIM : (h + 1) * HEAD_DIM],
+                        func=mybir.ActivationFunctionType.Exp,
+                        bias=neg_max_of[g][:, col : col + 1],
+                        accum_out=sums[:, col : col + 1],
+                    )
+            probs_of[g] = probs
+            sums_of[g] = sums
+
+        def stage_invert(g):
+            inverse = stats_pool.tile([P, TILES * HEADS], F32)
+            nc.vector.reciprocal(out=inverse[:], in_=sums_of[g][:])
+            inverse_of[g] = inverse
+            of_head_1 = inverse[:].rearrange("p (t h) -> p h t", h=HEADS)[:, 1, :]
+            nc.gpsimd.tensor_tensor(
+                out=probs_of[g][:, 1, :, :],
+                in0=probs_of[g][:, 1, :, :],
+                in1=of_head_1.unsqueeze(2).to_broadcast([P, TILES, HEAD_DIM]),
+                op=mybir.AluOpType.mult,
+            )
+
+        def stage_normalise(g):
+            probs = probs_of[g]
+            for t in range(TILES):
+                col = t * HEADS
+                nc.vector.tensor_scalar_mul(
+                    out=probs[:, 0, t, :],
+                    in0=probs[:, 0, t, :],
+                    scalar1=inverse_of[g][:, col : col + 1],
+                )
+            b, first_token = divmod(g * GROUP_TOKENS, BATCH_TOKENS)
+            nc.sync.dma_start(
+                out=out[b, :, first_token : first_token + GROUP_TOKENS, :].rearrange(
+                    "h (p t) d -> p h (t d)", t=TILES
+                ),
+                in_=probs[:].rearrange("p h t d -> p h (t d)"),
+            )
+
+        def run(stage, g):
+            if 0 <= g < GROUPS:
+                stage(g)
+
+        for step in range(GROUPS + 4):
+            run(stage_flip, step)
+            run(stage_project, step - 1)
+            run(stage_invert, step - 4)
+            run(stage_max, step - 2)
+            run(stage_copy, step)
+            run(stage_normalise, step - 4)
+            run(stage_exp, step - 3)

@@ -19,11 +19,16 @@ HEADS = 2
 HEAD_DIM = 128
 FEATURES = HEADS * HEAD_DIM
 TILES = 4
-TILES_PER_BANK = 2
-BANKS = TILES // TILES_PER_BANK
-GROUP_TOKENS = TILES * P
-GROUPS = TOKENS // GROUP_TOKENS
+BLOCK_TOKENS = TILES * P
+BLOCKS = TOKENS // BLOCK_TOKENS
+PAIR = 2
+
+GROUPS = [(block, 0, TILES) for block in range(BLOCKS - 1)] + [
+    (BLOCKS - 1, first, PAIR) for first in range(0, TILES, PAIR)
+]
 COPY_CYCLE = 4
+GPSIMD_TILES = 3
+PIECES = {0: [(0, 2), (2, 2)]}
 
 FLOPS = 2 * TOKENS * FEATURES * K
 
@@ -32,25 +37,37 @@ def tile_multiheadattention_pb_t_kernel(tc, Q, WQ, out):
     nc = tc.nc
     with ExitStack() as ctx:
         const = ctx.enter_context(tc.tile_pool(name="const", bufs=1))
-        rows_pool = ctx.enter_context(tc.tile_pool(name="rows", bufs=GROUPS))
+        rows_pool = ctx.enter_context(tc.tile_pool(name="rows", bufs=BLOCKS))
         operand_pool = ctx.enter_context(tc.tile_pool(name="operand", bufs=3))
-        stats_pool = ctx.enter_context(tc.tile_pool(name="stats", bufs=4))
-        probs_pool = ctx.enter_context(tc.tile_pool(name="probs", bufs=4))
-        flipped_pool = ctx.enter_context(tc.psum_pool(name="flipped", bufs=BANKS))
-        logits_pool = ctx.enter_context(tc.psum_pool(name="logits", bufs=3 * BANKS))
+        stats_pool = ctx.enter_context(tc.tile_pool(name="stats", bufs=6))
+        probs_pool = ctx.enter_context(tc.tile_pool(name="probs", bufs=len(GROUPS)))
+        flipped_pool = ctx.enter_context(tc.psum_pool(name="flipped", bufs=3))
+        logits_pool = ctx.enter_context(tc.psum_pool(name="logits", bufs=8 - 3))
         ctx.enter_context(tc.manual_schedule())
 
+        q_blocks = Q.flatten_outer_dims().rearrange("(b p t) k -> b p (t k)", p=P, t=TILES)
+        q_rows = []
+        for block in range(BLOCKS):
+            rows = rows_pool.tile([P, TILES * K], BF16)
+            q_rows.append(rows)
+
+        def load(block, piece):
+            first, n_tiles = piece
+            cols = slice(first * K, (first + n_tiles) * K)
+            nc.sync.dma_start(out=q_rows[block][:, cols], in_=q_blocks[block][:, cols])
+
         w_rows = const.tile([P, HEADS * K], BF16)
+        pieces = [
+            (block, piece) for block in range(BLOCKS) for piece in PIECES.get(block, [(0, TILES)])
+        ]
+        for block, piece in pieces[:2]:
+            load(block, piece)
         nc.sync.dma_start(
             out=w_rows[:].rearrange("p (h k) -> p h k", h=HEADS),
             in_=WQ.rearrange("(h p) k -> p h k", p=P),
         )
-        q_groups = Q.flatten_outer_dims().rearrange("(g p t) k -> g p (t k)", p=P, t=TILES)
-        q_rows = []
-        for g in range(GROUPS):
-            rows = rows_pool.tile([P, TILES * K], BF16)
-            nc.sync.dma_start(out=rows[:], in_=q_groups[g])
-            q_rows.append(rows)
+        for block, piece in pieces[2:]:
+            load(block, piece)
 
         ident = const.tile([P, P], F32)
         make_identity(nc, ident[:])
@@ -59,68 +76,78 @@ def tile_multiheadattention_pb_t_kernel(tc, Q, WQ, out):
         nc.vector.memset(warm[:], 0.0)
         nc.scalar.activation(out=warm[:], in_=warm[:], func=mybir.ActivationFunctionType.Exp)
 
-        def flip(rows, n_tiles):
-            words = rows[:].bitcast(F32).rearrange("p (j w) -> p j w", j=n_tiles)
-            banks = []
-            for first in range(0, n_tiles, TILES_PER_BANK):
-                flipped = flipped_pool.tile([P, TILES_PER_BANK, HALVES, P], F32)
-                for j in range(TILES_PER_BANK):
-                    for u in range(HALVES):
-                        nc.tensor.transpose(
-                            flipped[:, j, u, :],
-                            words[:, first + j, u :: HALVES],
-                            ident[:],
-                        )
-                banks.append(flipped)
-            return banks
+        def flip(words, n_tiles):
+            flipped = flipped_pool.tile([P, PAIR, HALVES, P], F32)
+            for j in range(n_tiles):
+                for u in range(HALVES):
+                    nc.tensor.transpose(flipped[:, j, u, :], words[:, j, u::HALVES], ident[:])
+            return flipped
 
-        def lay_side_by_side(banks, grouped, first_bank):
-            grouped_words = grouped[:].bitcast(F32).rearrange(
-                "p (i j r u) -> p i j r u", i=len(banks), j=TILES_PER_BANK, u=HALVES
+        def lay_side_by_side(copy_out, flipped, grouped, n_tiles):
+            copy_out(
+                out=grouped.bitcast(F32).rearrange("p (j r u) -> p j r u", j=n_tiles, u=HALVES),
+                in_=flipped[:, :n_tiles].rearrange("p j u r -> p j r u"),
             )
-            for i, flipped in enumerate(banks):
-                if (first_bank + i) % COPY_CYCLE == 1:
-                    copy_out = nc.vector.tensor_copy
-                else:
-                    copy_out = nc.scalar.copy
-                copy_out(out=grouped_words[:, i], in_=flipped[:].rearrange("p j u r -> p j r u"))
 
         w_grouped = const.tile([P, FEATURES * PACK], BF16, align_bytes=64)
         w_codes = const.tile([P, FEATURES], U32, align_bytes=64)
         w_scales = const.tile([P, FEATURES], U8, align_bytes=64)
-        lay_side_by_side(flip(w_rows, HEADS), w_grouped, 0)
-        nc.vector.quantize_mx(out=w_codes[:].bitcast(FP8X4), scales=w_scales[:], in_=w_grouped[:])
+        def prepare_w():
+            w_flipped = flip(w_rows[:].bitcast(F32).rearrange("p (j w) -> p j w", j=HEADS), HEADS)
+            lay_side_by_side(nc.vector.tensor_copy, w_flipped, w_grouped[:], HEADS)
+            nc.vector.quantize_mx(
+                out=w_codes[:].bitcast(FP8X4), scales=w_scales[:], in_=w_grouped[:]
+            )
 
         flipped_of = {}
         grouped_of = {}
-        codes_of = {}
         logits_of = {}
         neg_max_of = {}
         sums_of = {}
         probs_of = {}
         inverse_of = {}
 
-        def stage_flip(g):
-            flipped_of[g] = flip(q_rows[g], TILES)
+        def pairs_of(i):
+            n_tiles = GROUPS[i][2]
+            return [(t, min(PAIR, n_tiles - t)) for t in range(0, n_tiles, PAIR)]
 
-        def stage_copy(g):
-            grouped = operand_pool.tile([P, GROUP_TOKENS * PACK], BF16, align_bytes=64)
-            lay_side_by_side(flipped_of[g], grouped, g * BANKS)
-            grouped_of[g] = grouped
+        def stage_flip(i):
+            block, first, n_tiles = GROUPS[i]
+            words = q_rows[block][:].bitcast(F32).rearrange("p (t w) -> p t w", t=TILES)
+            banks = []
+            for t, n in pairs_of(i):
+                banks.append(flip(words[:, first + t : first + t + n, :], n))
+            flipped_of[i] = banks
+            if i == 0:
+                prepare_w()
 
-        def stage_project(g):
-            codes = operand_pool.tile([P, GROUP_TOKENS], U32, align_bytes=64)
-            scales = operand_pool.tile([P, GROUP_TOKENS], U8, align_bytes=64)
+        def stage_copy(i):
+            block, first, n_tiles = GROUPS[i]
+            width = P * PACK
+            grouped = operand_pool.tile([P, n_tiles * width], BF16, align_bytes=64)
+            for j, (t, n) in enumerate(pairs_of(i)):
+                lay_side_by_side(
+                    nc.vector.tensor_copy if (i * 2 + j) % COPY_CYCLE == 1 else nc.scalar.copy,
+                    flipped_of[i][j],
+                    grouped[:, t * width : (t + n) * width],
+                    n,
+                )
+            grouped_of[i] = grouped
+
+        def stage_project(i):
+            n_tiles = GROUPS[i][2]
+            codes = operand_pool.tile([P, n_tiles * P], U32, align_bytes=64)
+            scales = operand_pool.tile([P, n_tiles * P], U8, align_bytes=64)
             nc.vector.quantize_mx(
-                out=codes[:].bitcast(FP8X4), scales=scales[:], in_=grouped_of[g][:]
+                out=codes[:].bitcast(FP8X4), scales=scales[:], in_=grouped_of[i][:]
             )
             banks = []
-            for first in range(0, TILES, TILES_PER_BANK):
-                logits = logits_pool.tile([P, TILES_PER_BANK, FEATURES], F32)
-                for j in range(TILES_PER_BANK):
-                    tokens = slice((first + j) * P, (first + j + 1) * P)
+            for j, (first, n) in enumerate(pairs_of(i)):
+                logits = logits_pool.tile([P, PAIR, FEATURES], F32, name="logits")
+                for t in range(n):
+                    tokens = slice((first + t) * P, (first + t + 1) * P)
                     nc.tensor.matmul_mx(
-                        out=logits[:, j, :],
+                        out=logits[:, t, :],
                         lhsT=codes[:, tokens].bitcast(FP8X4),
                         lhsT_scale=scales[:, tokens],
                         rhs=w_codes[:].bitcast(FP8X4),
@@ -129,76 +156,86 @@ def tile_multiheadattention_pb_t_kernel(tc, Q, WQ, out):
                         stop=True,
                     )
                 banks.append(logits)
-            logits_of[g] = banks
+            logits_of[i] = banks
 
-        def stage_max(g):
-            neg_max = stats_pool.tile([P, TILES * HEADS], F32)
-            per_bank = TILES_PER_BANK * HEADS
-            for i, logits in enumerate(logits_of[g]):
+        def stage_max(i):
+            neg_max = stats_pool.tile([P, GROUPS[i][2] * HEADS], F32)
+            for j, (t, n) in enumerate(pairs_of(i)):
                 nc.vector.tensor_reduce(
-                    out=neg_max[:, i * per_bank : (i + 1) * per_bank],
-                    in_=logits[:].rearrange("p j (h d) -> p (j h) d", h=HEADS),
+                    out=neg_max[:, t * HEADS : (t + n) * HEADS],
+                    in_=logits_of[i][j][:, :n, :].rearrange("p j (h d) -> p (j h) d", h=HEADS),
                     axis=mybir.AxisListType.X,
                     op=mybir.AluOpType.max,
                     negate=True,
                 )
-            neg_max_of[g] = neg_max
+            neg_max_of[i] = neg_max
 
-        def stage_exp(g):
-            probs = probs_pool.tile([P, HEADS, TILES, HEAD_DIM], F32)
-            sums = stats_pool.tile([P, TILES * HEADS], F32)
-            for t in range(TILES):
-                logits = logits_of[g][t // TILES_PER_BANK]
+        def stage_exp(i):
+            n_tiles = GROUPS[i][2]
+            probs = probs_pool.tile([P, HEADS, n_tiles, HEAD_DIM], F32)
+            sums = stats_pool.tile([P, n_tiles * HEADS], F32)
+            for t in range(n_tiles):
+                logits = logits_of[i][t // PAIR]
                 for h in range(HEADS):
                     col = t * HEADS + h
                     nc.scalar.activation(
                         out=probs[:, h, t, :],
-                        in_=logits[:, t % TILES_PER_BANK, h * HEAD_DIM : (h + 1) * HEAD_DIM],
+                        in_=logits[:, t % PAIR, h * HEAD_DIM : (h + 1) * HEAD_DIM],
                         func=mybir.ActivationFunctionType.Exp,
-                        bias=neg_max_of[g][:, col : col + 1],
+                        bias=neg_max_of[i][:, col : col + 1],
                         accum_out=sums[:, col : col + 1],
                     )
-            probs_of[g] = probs
-            sums_of[g] = sums
+            probs_of[i] = probs
+            sums_of[i] = sums
 
-        def stage_invert(g):
-            inverse = stats_pool.tile([P, TILES * HEADS], F32)
-            nc.vector.reciprocal(out=inverse[:], in_=sums_of[g][:])
-            inverse_of[g] = inverse
-            of_head_1 = inverse[:].rearrange("p (t h) -> p h t", h=HEADS)[:, 1, :]
-            nc.gpsimd.tensor_tensor(
-                out=probs_of[g][:, 1, :, :],
-                in0=probs_of[g][:, 1, :, :],
-                in1=of_head_1.unsqueeze(2).to_broadcast([P, TILES, HEAD_DIM]),
-                op=mybir.AluOpType.mult,
-            )
+        def gpsimd_tiles(i):
+            return GPSIMD_TILES if i < len(GROUPS) - 4 else 0
 
-        def stage_normalise(g):
-            probs = probs_of[g]
-            for t in range(TILES):
-                col = t * HEADS
-                nc.vector.tensor_scalar_mul(
-                    out=probs[:, 0, t, :],
-                    in0=probs[:, 0, t, :],
-                    scalar1=inverse_of[g][:, col : col + 1],
+        def stage_invert(i):
+            n_tiles = GROUPS[i][2]
+            inverse = stats_pool.tile([P, n_tiles * HEADS], F32)
+            nc.vector.reciprocal(out=inverse[:], in_=sums_of[i][:])
+            inverse_of[i] = inverse
+            n_gpsimd = gpsimd_tiles(i)
+            if n_gpsimd:
+                probs = probs_of[i][:, 1, :n_gpsimd, :]
+                of_head_1 = inverse[:].rearrange("p (t h) -> p h t", h=HEADS)[:, 1, :n_gpsimd]
+                nc.gpsimd.tensor_tensor(
+                    out=probs,
+                    in0=probs,
+                    in1=of_head_1.unsqueeze(2).to_broadcast([P, n_gpsimd, HEAD_DIM]),
+                    op=mybir.AluOpType.mult,
                 )
-            b, first_token = divmod(g * GROUP_TOKENS, BATCH_TOKENS)
+
+        def stage_normalise(i):
+            block, first, n_tiles = GROUPS[i]
+            probs = probs_of[i]
+            for t in range(n_tiles):
+                for h in range(1 if t < gpsimd_tiles(i) else HEADS):
+                    col = t * HEADS + h
+                    nc.vector.tensor_scalar_mul(
+                        out=probs[:, h, t, :],
+                        in0=probs[:, h, t, :],
+                        scalar1=inverse_of[i][:, col : col + 1],
+                    )
+            batch, first_token = divmod(block * BLOCK_TOKENS, BATCH_TOKENS)
+            rows = out[batch, :, first_token : first_token + BLOCK_TOKENS, :]
             nc.sync.dma_start(
-                out=out[b, :, first_token : first_token + GROUP_TOKENS, :].rearrange(
-                    "h (p t) d -> p h (t d)", t=TILES
-                ),
-                in_=probs[:].rearrange("p h t d -> p h (t d)"),
+                out=rows.rearrange("h (p t) d -> p h t d", t=TILES)[
+                    :, :, first : first + n_tiles, :
+                ],
+                in_=probs[:],
             )
 
-        def run(stage, g):
-            if 0 <= g < GROUPS:
-                stage(g)
+        def run(stage, i):
+            if 0 <= i < len(GROUPS):
+                stage(i)
 
-        for step in range(GROUPS + 4):
-            run(stage_flip, step)
-            run(stage_project, step - 1)
-            run(stage_invert, step - 4)
-            run(stage_max, step - 2)
+        for step in range(-1, len(GROUPS) + 4):
+            run(stage_flip, step + 1)
             run(stage_copy, step)
-            run(stage_normalise, step - 4)
+            run(stage_invert, step - 4)
+            run(stage_project, step - 1)
+            run(stage_max, step - 2)
             run(stage_exp, step - 3)
+            run(stage_normalise, step - 4)

@@ -26,7 +26,7 @@ PAIR = 2
 GROUPS = [(block, 0, TILES) for block in range(BLOCKS - 1)] + [
     (BLOCKS - 1, first, PAIR) for first in range(0, TILES, PAIR)
 ]
-COPY_CYCLE = 4
+COPY_CYCLE = 8
 GPSIMD_TILES = 3
 PIECES = {0: [(0, 2), (2, 2)]}
 
@@ -127,7 +127,7 @@ def tile_multiheadattention_pb_t_kernel(tc, Q, WQ, out):
             grouped = operand_pool.tile([P, n_tiles * width], BF16, align_bytes=64)
             for j, (t, n) in enumerate(pairs_of(i)):
                 lay_side_by_side(
-                    nc.vector.tensor_copy if (i * 2 + j) % COPY_CYCLE == 1 else nc.scalar.copy,
+                    nc.vector.tensor_copy if (i * 2 + j) % COPY_CYCLE == COPY_CYCLE - 1 else nc.scalar.copy,
                     flipped_of[i][j],
                     grouped[:, t * width : (t + n) * width],
                     n,

@@ -24,11 +24,12 @@ BLOCKS = TOKENS // BLOCK_TOKENS
 PAIR = 2
 
 GROUPS = [(block, 0, TILES) for block in range(BLOCKS - 1)] + [
-    (BLOCKS - 1, first, PAIR) for first in range(0, TILES, PAIR)
+    (BLOCKS - 1, first, n_tiles) for first, n_tiles in ((0, 2), (2, 1), (3, 1))
 ]
-COPY_CYCLE = 8
+COPY_CYCLE = 5
+LAST_GROUPS = 5
 GPSIMD_TILES = 3
-PIECES = {0: [(0, 2), (2, 2)]}
+PIECES = {0: [(0, 2), (2, 2)], 1: [(0, 2), (2, 2)]}
 
 FLOPS = 2 * TOKENS * FEATURES * K
 
@@ -126,8 +127,10 @@ def tile_multiheadattention_pb_t_kernel(tc, Q, WQ, out):
             width = P * PACK
             grouped = operand_pool.tile([P, n_tiles * width], BF16, align_bytes=64)
             for j, (t, n) in enumerate(pairs_of(i)):
+                bank = i * (TILES // PAIR) + j
+                by_vector = bank % COPY_CYCLE == COPY_CYCLE - 1 and i < len(GROUPS) - LAST_GROUPS
                 lay_side_by_side(
-                    nc.vector.tensor_copy if (i * 2 + j) % COPY_CYCLE == COPY_CYCLE - 1 else nc.scalar.copy,
+                    nc.vector.tensor_copy if by_vector else nc.scalar.copy,
                     flipped_of[i][j],
                     grouped[:, t * width : (t + n) * width],
                     n,
@@ -189,7 +192,7 @@ def tile_multiheadattention_pb_t_kernel(tc, Q, WQ, out):
             sums_of[i] = sums
 
         def gpsimd_tiles(i):
-            return GPSIMD_TILES if i < len(GROUPS) - 4 else 0
+            return GPSIMD_TILES if i < len(GROUPS) - LAST_GROUPS else 0
 
         def stage_invert(i):
             n_tiles = GROUPS[i][2]

@@ -29,6 +29,8 @@ GROUPS = [(block, 0, TILES) for block in range(BLOCKS - 1)] + [
 COPY_CYCLE = 5
 LAST_GROUPS = 5
 GPSIMD_TILES = 3
+WARM_COLUMNS = 512
+WARM_PASSES = 6
 PIECES = {0: [(0, 2), (2, 2)], 1: [(0, 2), (2, 2)]}
 
 FLOPS = 2 * TOKENS * FEATURES * K
@@ -76,6 +78,14 @@ def tile_multiheadattention_pb_t_kernel(tc, Q, WQ, out):
         warm = const.tile([P, 1], F32)
         nc.vector.memset(warm[:], 0.0)
         nc.scalar.activation(out=warm[:], in_=warm[:], func=mybir.ActivationFunctionType.Exp)
+
+        zeros = const.tile([P, WARM_COLUMNS], BF16)
+        nc.vector.memset(zeros[:], 0.0)
+        warm_sums = logits_pool.tile([P, WARM_COLUMNS], F32, name="logits")
+        for warm_pass in range(WARM_PASSES):
+            nc.tensor.matmul(
+                out=warm_sums[:], lhsT=zeros[:, :P], rhs=zeros[:], start=True, stop=True
+            )
 
         def flip(words, n_tiles):
             flipped = flipped_pool.tile([P, PAIR, HALVES, P], F32)

from contextlib import ExitStack

import concourse.mybir as mybir
from concourse.masks import make_identity

F32 = mybir.dt.float32
BF16 = mybir.dt.bfloat16
U32 = mybir.dt.uint32
U8 = mybir.dt.uint8
FP8X4 = mybir.dt.float8_e4m3fn_x4

P = 128
PACK = 4
HALVES = 2
TOKENS = 4 * 2048
BATCH_TOKENS = 2048
K = 512
HEADS = 2
HEAD_DIM = 128
FEATURES = HEADS * HEAD_DIM
TILES = 4
BLOCK_TOKENS = TILES * P
BLOCKS = TOKENS // BLOCK_TOKENS
PAIR = 2

GROUPS = [(block, 0, TILES) for block in range(BLOCKS - 1)] + [
    (BLOCKS - 1, first, n_tiles) for first, n_tiles in ((0, 2), (2, 1), (3, 1))
]
COPY_CYCLE = 5
LAST_GROUPS = 5
GPSIMD_TILES = 3
WARM_COLUMNS = 512
WARM_PASSES = 6
PIECES = {0: [(0, 2), (2, 2)], 1: [(0, 2), (2, 2)]}

FLOPS = 2 * TOKENS * FEATURES * K


def tile_multiheadattention_pb_t_kernel(tc, Q, WQ, out):
    nc = tc.nc
    with ExitStack() as ctx:
        const = ctx.enter_context(tc.tile_pool(name="const", bufs=1))
        rows_pool = ctx.enter_context(tc.tile_pool(name="rows", bufs=BLOCKS))
        operand_pool = ctx.enter_context(tc.tile_pool(name="operand", bufs=3))
        stats_pool = ctx.enter_context(tc.tile_pool(name="stats", bufs=6))
        probs_pool = ctx.enter_context(tc.tile_pool(name="probs", bufs=len(GROUPS)))
        flipped_pool = ctx.enter_context(tc.psum_pool(name="flipped", bufs=3))
        logits_pool = ctx.enter_context(tc.psum_pool(name="logits", bufs=8 - 3))
        ctx.enter_context(tc.manual_schedule())

        q_blocks = Q.flatten_outer_dims().rearrange("(b p t) k -> b p (t k)", p=P, t=TILES)
        q_rows = []
        for block in range(BLOCKS):
            rows = rows_pool.tile([P, TILES * K], BF16)
            q_rows.append(rows)

        def load(block, piece):
            first, n_tiles = piece
            cols = slice(first * K, (first + n_tiles) * K)
            nc.sync.dma_start(out=q_rows[block][:, cols], in_=q_blocks[block][:, cols])

        w_rows = const.tile([P, HEADS * K], BF16)
        pieces = [
            (block, piece) for block in range(BLOCKS) for piece in PIECES.get(block, [(0, TILES)])
        ]
        for block, piece in pieces[:2]:
            load(block, piece)
        nc.sync.dma_start(
            out=w_rows[:].rearrange("p (h k) -> p h k", h=HEADS),
            in_=WQ.rearrange("(h p) k -> p h k", p=P),
        )
        for block, piece in pieces[2:]:
            load(block, piece)

        ident = const.tile([P, P], F32)
        make_identity(nc, ident[:])

        warm = const.tile([P, 1], F32)
        nc.vector.memset(warm[:], 0.0)
        nc.scalar.activation(out=warm[:], in_=warm[:], func=mybir.ActivationFunctionType.Exp)

        zeros = const.tile([P, WARM_COLUMNS], BF16)
        nc.vector.memset(zeros[:], 0.0)
        warm_sums = logits_pool.tile([P, WARM_COLUMNS], F32, name="logits")
        for warm_pass in range(WARM_PASSES):
            nc.tensor.matmul(
                out=warm_sums[:], lhsT=zeros[:, :P], rhs=zeros[:], start=True, stop=True
            )

        def flip(words, n_tiles):
            flipped = flipped_pool.tile([P, PAIR, HALVES, P], F32)
            for j in range(n_tiles):
                for u in range(HALVES):
                    nc.tensor.transpose(flipped[:, j, u, :], words[:, j, u::HALVES], ident[:])
            return flipped

        def lay_side_by_side(copy_out, flipped, grouped, n_tiles):
            copy_out(
                out=grouped.bitcast(F32).rearrange("p (j r u) -> p j r u", j=n_tiles, u=HALVES),
                in_=flipped[:, :n_tiles].rearrange("p j u r -> p j r u"),
            )

        w_grouped = const.tile([P, FEATURES * PACK], BF16, align_bytes=64)
        w_codes = const.tile([P, FEATURES], U32, align_bytes=64)
        w_scales = const.tile([P, FEATURES], U8, align_bytes=64)
        def prepare_w():
            w_flipped = flip(w_rows[:].bitcast(F32).rearrange("p (j w) -> p j w", j=HEADS), HEADS)
            lay_side_by_side(nc.vector.tensor_copy, w_flipped, w_grouped[:], HEADS)
            nc.vector.quantize_mx(
                out=w_codes[:].bitcast(FP8X4), scales=w_scales[:], in_=w_grouped[:]
            )

        flipped_of = {}
        grouped_of = {}
        logits_of = {}
        neg_max_of = {}
        sums_of = {}
        probs_of = {}
        inverse_of = {}

        def pairs_of(i):
            n_tiles = GROUPS[i][2]
            return [(t, min(PAIR, n_tiles - t)) for t in range(0, n_tiles, PAIR)]

        def stage_flip(i):
            block, first, n_tiles = GROUPS[i]
            words = q_rows[block][:].bitcast(F32).rearrange("p (t w) -> p t w", t=TILES)
            banks = []
            for t, n in pairs_of(i):
                banks.append(flip(words[:, first + t : first + t + n, :], n))
            flipped_of[i] = banks
            if i == 0:
                prepare_w()

        def stage_copy(i):
            block, first, n_tiles = GROUPS[i]
            width = P * PACK
            grouped = operand_pool.tile([P, n_tiles * width], BF16, align_bytes=64)
            for j, (t, n) in enumerate(pairs_of(i)):
                bank = i * (TILES // PAIR) + j
                by_vector = bank % COPY_CYCLE == COPY_CYCLE - 1 and i < len(GROUPS) - LAST_GROUPS
                lay_side_by_side(
                    nc.vector.tensor_copy if by_vector else nc.scalar.copy,
                    flipped_of[i][j],
                    grouped[:, t * width : (t + n) * width],
                    n,
                )
            grouped_of[i] = grouped

        def stage_project(i):
            n_tiles = GROUPS[i][2]
            codes = operand_pool.tile([P, n_tiles * P], U32, align_bytes=64)
            scales = operand_pool.tile([P, n_tiles * P], U8, align_bytes=64)
            nc.vector.quantize_mx(
                out=codes[:].bitcast(FP8X4), scales=scales[:], in_=grouped_of[i][:]
            )
            banks = []
            for j, (first, n) in enumerate(pairs_of(i)):
                logits = logits_pool.tile([P, PAIR, FEATURES], F32, name="logits")
                for t in range(n):
                    tokens = slice((first + t) * P, (first + t + 1) * P)
                    nc.tensor.matmul_mx(
                        out=logits[:, t, :],
                        lhsT=codes[:, tokens].bitcast(FP8X4),
                        lhsT_scale=scales[:, tokens],
                        rhs=w_codes[:].bitcast(FP8X4),
                        rhs_scale=w_scales[:],
                        start=True,
                        stop=True,
                    )
                banks.append(logits)
            logits_of[i] = banks

        def stage_max(i):
            neg_max = stats_pool.tile([P, GROUPS[i][2] * HEADS], F32)
            for j, (t, n) in enumerate(pairs_of(i)):
                nc.vector.tensor_reduce(
                    out=neg_max[:, t * HEADS : (t + n) * HEADS],
                    in_=logits_of[i][j][:, :n, :].rearrange("p j (h d) -> p (j h) d", h=HEADS),
                    axis=mybir.AxisListType.X,
                    op=mybir.AluOpType.max,
                    negate=True,
                )
            neg_max_of[i] = neg_max

        def stage_exp(i):
            n_tiles = GROUPS[i][2]
            probs = probs_pool.tile([P, HEADS, n_tiles, HEAD_DIM], F32)
            sums = stats_pool.tile([P, n_tiles * HEADS], F32)
            for t in range(n_tiles):
                logits = logits_of[i][t // PAIR]
                for h in range(HEADS):
                    col = t * HEADS + h
                    nc.scalar.activation(
                        out=probs[:, h, t, :],
                        in_=logits[:, t % PAIR, h * HEAD_DIM : (h + 1) * HEAD_DIM],
                        func=mybir.ActivationFunctionType.Exp,
                        bias=neg_max_of[i][:, col : col + 1],
                        accum_out=sums[:, col : col + 1],
                    )
            probs_of[i] = probs
            sums_of[i] = sums

        def gpsimd_tiles(i):
            return GPSIMD_TILES if i < len(GROUPS) - LAST_GROUPS else 0

        def stage_invert(i):
            n_tiles = GROUPS[i][2]
            inverse = stats_pool.tile([P, n_tiles * HEADS], F32)
            nc.vector.reciprocal(out=inverse[:], in_=sums_of[i][:])
            inverse_of[i] = inverse
            n_gpsimd = gpsimd_tiles(i)
            if n_gpsimd:
                probs = probs_of[i][:, 1, :n_gpsimd, :]
                of_head_1 = inverse[:].rearrange("p (t h) -> p h t", h=HEADS)[:, 1, :n_gpsimd]
                nc.gpsimd.tensor_tensor(
                    out=probs,
                    in0=probs,
                    in1=of_head_1.unsqueeze(2).to_broadcast([P, n_gpsimd, HEAD_DIM]),
                    op=mybir.AluOpType.mult,
                )

        def stage_normalise(i):
            block, first, n_tiles = GROUPS[i]
            probs = probs_of[i]
            for t in range(n_tiles):
                for h in range(1 if t < gpsimd_tiles(i) else HEADS):
                    col = t * HEADS + h
                    nc.vector.tensor_scalar_mul(
                        out=probs[:, h, t, :],
                        in0=probs[:, h, t, :],
                        scalar1=inverse_of[i][:, col : col + 1],
                    )
            batch, first_token = divmod(block * BLOCK_TOKENS, BATCH_TOKENS)
            rows = out[batch, :, first_token : first_token + BLOCK_TOKENS, :]
            nc.sync.dma_start(
                out=rows.rearrange("h (p t) d -> p h t d", t=TILES)[
                    :, :, first : first + n_tiles, :
                ],
                in_=probs[:],
            )

        def run(stage, i):
            if 0 <= i < len(GROUPS):
                stage(i)

        for step in range(-1, len(GROUPS) + 4):
            run(stage_flip, step + 1)
            run(stage_copy, step)
            run(stage_invert, step - 4)
            run(stage_project, step - 1)
            run(stage_max, step - 2)
            run(stage_exp, step - 3)
            run(stage_normalise, step - 4)
